import numpy as np
import ml_dtypes


def mxq(x, axis, fmt="e4m3"):
    dtype, down = {"e4m3": (ml_dtypes.float8_e4m3fn, 7), "e5m2": (ml_dtypes.float8_e5m2, 14)}[fmt]
    v = np.moveaxis(np.asarray(x, np.float32).astype(ml_dtypes.bfloat16).astype(np.float64), axis, -1)
    blocks = v.reshape(v.shape[:-1] + (-1, 32))
    amax = np.abs(blocks).max(-1, keepdims=True)
    byte = np.maximum(np.where(amax > 0, np.frexp(amax)[1] - 1 + 127, 0) - down, 1)
    scale = np.exp2(byte - 127.0)
    codes = (blocks / scale).astype(np.float32).astype(dtype).astype(np.float64)
    return np.moveaxis((codes * scale).reshape(v.shape), -1, axis)


WIDE = False


def mx_kscale(k):
    if not WIDE:
        return np.ones(k)
    levels = np.array([10, -10, 5, -5, 0])
    a = np.random.permutation(np.resize(levels, k // 512 * 4)).reshape(k // 512, 4)
    idx = np.arange(k)
    return np.exp2(a[idx // 512, idx % 128 // 32])


BF16 = ml_dtypes.bfloat16


def bf(x):
    return np.asarray(x, np.float32).astype(BF16)


def f64(x):
    return np.asarray(x).astype(np.float64)


B, T, E = 2, 1024, 512


def setup_inputs():
    s, t = mx_kscale(E), mx_kscale(E)
    r = np.random.standard_normal
    return {"x1": bf(r((B, T, E)) * s), "x2": bf(r((B, T, E)) * s),
            "W1": bf(r((E, E)) * 0.4 / np.sqrt(E) / s[:, None] * t), "W2": bf(r((E, E)) * 0.4 / np.sqrt(E) / s[:, None] / t),
            "b1": bf(r((T, E)) * 0.1 * t), "b2": bf(r((T, E)) * 0.1 / t)}


def reference(x1, x2, W1, W2, b1, b2):
    e1t = np.maximum((mxq(f64(x1), 2, "e4m3") @ mxq(f64(W1), 0, "e4m3")) + f64(b1), 0.0)
    e2t = np.maximum((mxq(f64(x2), 2, "e4m3") @ mxq(f64(W2), 0, "e4m3")) + f64(b2), 0.0)
    scores = mxq(e2t, 2, "e4m3") @ mxq(e1t, 2, "e4m3").transpose(0, 2, 1)
    ex = np.exp(scores - scores.max(-1, keepdims=True))
    return ex / ex.sum(-1, keepdims=True)

@@ -1,0 +1,234 @@
+from contextlib import ExitStack
+
+import concourse.bass as bass
+import concourse.mybir as mybir
+import concourse.tile as tile
+from concourse.masks import make_identity
+
+F32 = mybir.dt.float32
+BF16 = mybir.dt.bfloat16
+U32 = mybir.dt.uint32
+U8 = mybir.dt.uint8
+FP8X4 = mybir.dt.float8_e4m3fn_x4
+ALU = mybir.AluOpType
+ACT = mybir.ActivationFunctionType
+AX = mybir.AxisListType
+
+B, T, E = 2, 1024, 512
+P = 128
+UNIT = 512
+FLOPS = 2 * (2 * B * T * E * E) + 2 * B * T * T * E
+FMAX = 3.4028234663852886e38
+
+
+def tile_attentionmm_pa_kernel(tc, x1, x2, W1, W2, b1, b2, out):
+    nc = tc.nc
+    with ExitStack() as ctx:
+        keep = ctx.enter_context(tc.tile_pool(name="keep", bufs=1))
+        work = ctx.enter_context(tc.tile_pool(name="work", bufs=3))
+        expool = ctx.enter_context(tc.tile_pool(name="expool", bufs=5))
+        small = ctx.enter_context(tc.tile_pool(name="small", bufs=6))
+        psum = ctx.enter_context(tc.psum_pool(name="psum", bufs=8))
+
+        ident = keep.tile([P, P], F32, name="ident")
+        make_identity(nc, ident[:])
+        warm = keep.tile([P, 1], F32, name="warm")
+        nc.vector.memset(warm[:], 0.0)
+        nc.scalar.activation(out=warm[:], in_=warm[:], func=ACT.Exp)
+
+        xs = {1: x1, 2: x2}
+        ws = {1: W1, 2: W2}
+        bs = {1: b1, 2: b2}
+        x_view = {
+            1: x1.rearrange("b (n p) k -> p b n k", p=P),
+            2: x2.rearrange("b (p n) k -> p b n k", p=P),
+        }
+        b_view = {
+            1: b1.rearrange("(n p) f -> p n f", p=P),
+            2: b2.rearrange("(p n) f -> p n f", p=P),
+        }
+        out_view = out.rearrange("b (p n) j -> p b n j", p=P)
+
+        x_sb, b_sb, w_sb, wg, w_codes, w_scales = {}, {}, {}, {}, {}, {}
+        x_codes, x_scales, bT, e_codes, e_scales = {}, {}, {}, {}, {}
+        for s in (1, 2):
+            x_sb[s] = keep.tile([P, B, 8, E], BF16, name="x_sb%d" % s)
+            b_sb[s] = keep.tile([P, 8, E], BF16, name="b_sb%d" % s)
+            w_sb[s] = keep.tile([P, 4, E], BF16, name="w_sb%d" % s)
+            wg[s] = keep.tile([P, E, 4], BF16, name="wg%d" % s, align_bytes=64)
+            w_codes[s] = keep.tile([P, E], U32, name="w_codes%d" % s, align_bytes=64)
+            w_scales[s] = keep.tile([P, E], U8, name="w_scales%d" % s, align_bytes=64)
+            x_codes[s] = keep.tile([P, B * T], U32, name="x_codes%d" % s, align_bytes=64)
+            x_scales[s] = keep.tile([P, B * T], U8, name="x_scales%d" % s, align_bytes=64)
+            bT[s] = keep.tile([P, T, 4], BF16, name="bT%d" % s, align_bytes=64)
+            e_codes[s] = keep.tile([P, B * T], U32, name="e_codes%d" % s, align_bytes=64)
+            e_scales[s] = keep.tile([P, B * T], U8, name="e_scales%d" % s, align_bytes=64)
+
+        def load_w(s):
+            nc.sync.dma_start(
+                out=w_sb[s][:].rearrange("q (u e) c -> q u e c", u=2),
+                in_=ws[s].rearrange("(u q e) c -> q u e c", u=2, e=2),
+            )
+
+        def load_x(s, b, h):
+            nc.sync.dma_start(out=x_sb[s][:, b, 4 * h : 4 * h + 4, :], in_=x_view[s][:, b, 4 * h : 4 * h + 4, :])
+
+        def load_b(s, h):
+            nc.sync.dma_start(out=b_sb[s][:, 4 * h : 4 * h + 4, :], in_=b_view[s][:, 4 * h : 4 * h + 4, :])
+
+        def prep_w(s):
+            for u in range(2):
+                nc.vector.tensor_copy(
+                    out=wg[s][:, 256 * u : 256 * u + 256, :].rearrange("q (e p) s -> q e p s", e=2),
+                    in_=w_sb[s][:, :, 256 * u : 256 * u + 256].rearrange("q s (p e) -> q e p s", e=2),
+                )
+            nc.vector.quantize_mx(
+                out=w_codes[s][:].bitcast(FP8X4),
+                scales=w_scales[s][:],
+                in_=wg[s][:].rearrange("q f s -> q (f s)"),
+            )
+
+        def transpose_unit(src, dst):
+            dst_words = dst.rearrange("p t j -> p (t j)").bitcast(F32).rearrange("p (t u) -> p t u", u=2)
+            for pr in range(2):
+                ps = psum.tile([P, 512], F32, name="tp", tag="bank")
+                psv = ps[:].rearrange("p (a u t) -> p a u t", a=2, u=2)
+                for a in range(2):
+                    words = src[:, 2 * pr + a, :].bitcast(F32)
+                    for u in range(2):
+                        nc.tensor.transpose(psv[:, a, u, :], words[:, P * u : P * u + P], ident[:])
+                nc.scalar.copy(
+                    out=dst_words[:, 256 * pr : 256 * pr + 256, :].rearrange("p (a t) u -> p a t u", a=2),
+                    in_=psv.rearrange("p a u t -> p a t u"),
+                )
+
+        def x_unit(s, b, h):
+            xg = work.tile([P, UNIT, 4], BF16, name="xg", tag="xg", align_bytes=64)
+            transpose_unit(x_sb[s][:, b, 4 * h : 4 * h + 4, :], xg[:])
+            c0 = b * T + h * UNIT
+            nc.vector.quantize_mx(
+                out=x_codes[s][:, c0 : c0 + UNIT].bitcast(FP8X4),
+                scales=x_scales[s][:, c0 : c0 + UNIT],
+                in_=xg[:].rearrange("p t j -> p (t j)"),
+            )
+
+        def bias_unit(s, h):
+            transpose_unit(b_sb[s][:, 4 * h : 4 * h + 4, :], bT[s][:, h * UNIT : h * UNIT + UNIT, :])
+
+        def stage1_unit(s, b, h):
+            c0 = b * T + h * UNIT
+            pre = work.tile([P, UNIT, 4], BF16, name="pre", tag="pre", align_bytes=64)
+            for tt in range(4):
+                ps = psum.tile([P, 512], F32, name="s1", tag="bank")
+                psv = ps[:].rearrange("p (j t) -> p j t", j=4)
+                for j in range(4):
+                    nc.tensor.matmul_mx(
+                        out=psv[:, j, :],
+                        lhsT=w_codes[s][:, P * j : P * j + P].bitcast(FP8X4),
+                        lhsT_scale=w_scales[s][:, P * j : P * j + P],
+                        rhs=x_codes[s][:, c0 + P * tt : c0 + P * tt + P].bitcast(FP8X4),
+                        rhs_scale=x_scales[s][:, c0 + P * tt : c0 + P * tt + P],
+                        start=True,
+                        stop=True,
+                    )
+                nc.vector.tensor_tensor(
+                    out=pre[:, P * tt : P * tt + P, :],
+                    in0=psv.rearrange("p j t -> p t j"),
+                    in1=bT[s][:, h * UNIT + P * tt : h * UNIT + P * tt + P, :],
+                    op=ALU.add,
+                )
+            flat = pre[:].rearrange("p t j -> p (t j)")
+            nc.gpsimd.tensor_scalar(out=flat, in0=flat, scalar1=FMAX, scalar2=0.0, op0=ALU.min, op1=ALU.max)
+            nc.vector.quantize_mx(
+                out=e_codes[s][:, c0 : c0 + UNIT].bitcast(FP8X4),
+                scales=e_scales[s][:, c0 : c0 + UNIT],
+                in_=flat,
+            )
+
+        def stage2_tile(b, n):
+            i0 = b * T + P * n
+            banks = []
+            part = small.tile([P, 2], F32, name="part", tag="part")
+            for hh in range(2):
+                sc = psum.tile([P, 512], F32, name="sc", tag="bank")
+                j0 = b * T + 512 * hh
+                nc.tensor.matmul_mx(
+                    out=sc[:],
+                    lhsT=e_codes[2][:, i0 : i0 + P].bitcast(FP8X4),
+                    lhsT_scale=e_scales[2][:, i0 : i0 + P],
+                    rhs=e_codes[1][:, j0 : j0 + 512].bitcast(FP8X4),
+                    rhs_scale=e_scales[1][:, j0 : j0 + 512],
+                    start=True,
+                    stop=True,
+                )
+                nc.vector.tensor_reduce(out=part[:, hh : hh + 1], in_=sc[:], axis=AX.X, op=ALU.max)
+                banks.append(sc)
+            negm = small.tile([P, 1], F32, name="negm", tag="negm")
+            nc.vector.tensor_reduce(out=negm[:], in_=part[:], axis=AX.X, op=ALU.max, negate=True)
+            ex = expool.tile([P, T], F32, name="ex", tag="ex")
+            sums = small.tile([P, 2], F32, name="sums", tag="sums")
+            for hh in range(2):
+                nc.scalar.activation(
+                    out=ex[:, 512 * hh : 512 * hh + 512],
+                    in_=banks[hh][:],
+                    func=ACT.Exp,
+                    bias=negm[:, 0:1],
+                    scale=1.0,
+                    accum_out=sums[:, hh : hh + 1],
+                )
+            tot = small.tile([P, 1], F32, name="tot", tag="tot")
+            nc.vector.tensor_reduce(out=tot[:], in_=sums[:], axis=AX.X, op=ALU.add)
+            rs = small.tile([P, 1], F32, name="rs", tag="rs")
+            nc.vector.reciprocal(out=rs[:], in_=tot[:])
+            nc.gpsimd.tensor_scalar(out=ex[:], in0=ex[:], scalar1=rs[:, 0:1], scalar2=0.0, op0=ALU.mult, op1=ALU.add)
+            nc.sync.dma_start(out=out_view[:, b, n, :], in_=ex[:])
+
+        load_w(1)
+        load_x(1, 0, 0)
+        load_b(1, 0)
+        load_x(1, 0, 1)
+        load_b(1, 1)
+        load_w(2)
+        load_x(2, 0, 0)
+        load_b(2, 0)
+        load_x(2, 0, 1)
+        load_b(2, 1)
+        load_x(1, 1, 0)
+        load_x(1, 1, 1)
+        load_x(2, 1, 0)
+        load_x(2, 1, 1)
+
+        prep_w(1)
+        x_unit(1, 0, 0)
+        bias_unit(1, 0)
+        stage1_unit(1, 0, 0)
+        x_unit(1, 0, 1)
+        bias_unit(1, 1)
+        stage1_unit(1, 0, 1)
+        prep_w(2)
+        x_unit(2, 0, 0)
+        bias_unit(2, 0)
+        stage1_unit(2, 0, 0)
+        stage2_tile(0, 0)
+        stage2_tile(0, 1)
+        x_unit(2, 0, 1)
+        bias_unit(2, 1)
+        stage1_unit(2, 0, 1)
+        stage2_tile(0, 2)
+        stage2_tile(0, 3)
+        x_unit(1, 1, 0)
+        stage1_unit(1, 1, 0)
+        stage2_tile(0, 4)
+        stage2_tile(0, 5)
+        x_unit(1, 1, 1)
+        stage1_unit(1, 1, 1)
+        stage2_tile(0, 6)
+        stage2_tile(0, 7)
+        x_unit(2, 1, 0)
+        stage1_unit(2, 1, 0)
+        stage2_tile(1, 0)
+        stage2_tile(1, 1)
+        x_unit(2, 1, 1)
+        stage1_unit(2, 1, 1)
+        for n in range(2, 8):
+            stage2_tile(1, n)

@@ -1,8 +1,6 @@
 from contextlib import ExitStack
 
-import concourse.bass as bass
 import concourse.mybir as mybir
-import concourse.tile as tile
 from concourse.masks import make_identity
 
 F32 = mybir.dt.float32
@@ -16,29 +14,23 @@ AX = mybir.AxisListType
 
 B, T, E = 2, 1024, 512
 P = 128
-UNIT = 512
+HU = 256
 FLOPS = 2 * (2 * B * T * E * E) + 2 * B * T * T * E
-FMAX = 3.4028234663852886e38
+PIN = True
 
 
 def tile_attentionmm_pa_kernel(tc, x1, x2, W1, W2, b1, b2, out):
     nc = tc.nc
     with ExitStack() as ctx:
+        if PIN:
+            ctx.enter_context(tc.manual_schedule())
         keep = ctx.enter_context(tc.tile_pool(name="keep", bufs=1))
-        work = ctx.enter_context(tc.tile_pool(name="work", bufs=3))
-        expool = ctx.enter_context(tc.tile_pool(name="expool", bufs=5))
-        small = ctx.enter_context(tc.tile_pool(name="small", bufs=6))
-        psum = ctx.enter_context(tc.psum_pool(name="psum", bufs=8))
+        work = ctx.enter_context(tc.tile_pool(name="work", bufs=4))
+        expool = ctx.enter_context(tc.tile_pool(name="expool", bufs=6))
+        small = ctx.enter_context(tc.tile_pool(name="small", bufs=8))
+        psum = ctx.enter_context(tc.psum_pool(name="psum", bufs=2))
 
-        ident = keep.tile([P, P], F32, name="ident")
-        make_identity(nc, ident[:])
-        warm = keep.tile([P, 1], F32, name="warm")
-        nc.vector.memset(warm[:], 0.0)
-        nc.scalar.activation(out=warm[:], in_=warm[:], func=ACT.Exp)
-
-        xs = {1: x1, 2: x2}
         ws = {1: W1, 2: W2}
-        bs = {1: b1, 2: b2}
         x_view = {
             1: x1.rearrange("b (n p) k -> p b n k", p=P),
             2: x2.rearrange("b (p n) k -> p b n k", p=P),
@@ -70,90 +62,135 @@ def tile_attentionmm_pa_kernel(tc, x1, x2, W1, W2, b1, b2, out):
                 in_=ws[s].rearrange("(u q e) c -> q u e c", u=2, e=2),
             )
 
-        def load_x(s, b, h):
-            nc.sync.dma_start(out=x_sb[s][:, b, 4 * h : 4 * h + 4, :], in_=x_view[s][:, b, 4 * h : 4 * h + 4, :])
+        def load_x(s, b, n0, n1):
+            nc.sync.dma_start(out=x_sb[s][:, b, n0:n1, :], in_=x_view[s][:, b, n0:n1, :])
 
-        def load_b(s, h):
-            nc.sync.dma_start(out=b_sb[s][:, 4 * h : 4 * h + 4, :], in_=b_view[s][:, 4 * h : 4 * h + 4, :])
+        def load_b(s, n0, n1):
+            nc.sync.dma_start(out=b_sb[s][:, n0:n1, :], in_=b_view[s][:, n0:n1, :])
 
-        def prep_w(s):
+        load_w(1)
+        for q in range(4):
+            load_x(1, 0, 2 * q, 2 * q + 2)
+            load_b(1, 2 * q, 2 * q + 2)
+        load_w(2)
+        for h in range(2):
+            load_x(2, 0, 4 * h, 4 * h + 4)
+            load_b(2, 4 * h, 4 * h + 4)
+        load_x(1, 1, 0, 8)
+        load_x(2, 1, 0, 8)
+
+        ident = keep.tile([P, P], F32, name="ident")
+        make_identity(nc, ident[:])
+        warm = keep.tile([P, 1], F32, name="warm")
+        nc.vector.memset(warm[:], 0.0)
+        nc.scalar.activation(out=warm[:], in_=warm[:], func=ACT.Exp)
+
+        units = [(s, b, q) for b in range(B) for s in (1, 2) for q in range(4)]
+        xg, pre, s1, sc, part, negm, ex, sums, tot, rs = {}, {}, {}, {}, {}, {}, {}, {}, {}, {}
+
+        def regroup_w(s, copy):
             for u in range(2):
-                nc.vector.tensor_copy(
+                copy(
                     out=wg[s][:, 256 * u : 256 * u + 256, :].rearrange("q (e p) s -> q e p s", e=2),
                     in_=w_sb[s][:, :, 256 * u : 256 * u + 256].rearrange("q s (p e) -> q e p s", e=2),
                 )
+
+        def quantise_w(s):
             nc.vector.quantize_mx(
                 out=w_codes[s][:].bitcast(FP8X4),
                 scales=w_scales[s][:],
                 in_=wg[s][:].rearrange("q f s -> q (f s)"),
             )
 
-        def transpose_unit(src, dst):
-            dst_words = dst.rearrange("p t j -> p (t j)").bitcast(F32).rearrange("p (t u) -> p t u", u=2)
-            for pr in range(2):
-                ps = psum.tile([P, 512], F32, name="tp", tag="bank")
-                psv = ps[:].rearrange("p (a u t) -> p a u t", a=2, u=2)
-                for a in range(2):
-                    words = src[:, 2 * pr + a, :].bitcast(F32)
-                    for u in range(2):
-                        nc.tensor.transpose(psv[:, a, u, :], words[:, P * u : P * u + P], ident[:])
-                nc.scalar.copy(
-                    out=dst_words[:, 256 * pr : 256 * pr + 256, :].rearrange("p (a t) u -> p a t u", a=2),
-                    in_=psv.rearrange("p a u t -> p a t u"),
-                )
-
-        def x_unit(s, b, h):
-            xg = work.tile([P, UNIT, 4], BF16, name="xg", tag="xg", align_bytes=64)
-            transpose_unit(x_sb[s][:, b, 4 * h : 4 * h + 4, :], xg[:])
-            c0 = b * T + h * UNIT
-            nc.vector.quantize_mx(
-                out=x_codes[s][:, c0 : c0 + UNIT].bitcast(FP8X4),
-                scales=x_scales[s][:, c0 : c0 + UNIT],
-                in_=xg[:].rearrange("p t j -> p (t j)"),
+        def transposed(src, dst):
+            ps = psum.tile([P, 512], F32, name="tp", tag="tp")
+            psv = ps[:].rearrange("p (a u t) -> p a u t", a=2, u=2)
+            for a in range(2):
+                words = src[:, a, :].bitcast(F32)
+                for u in range(2):
+                    nc.tensor.transpose(psv[:, a, u, :], words[:, P * u : P * u + P], ident[:])
+            nc.scalar.copy(
+                out=dst.rearrange("p t j -> p (t j)").bitcast(F32).rearrange("p (a t u) -> p a t u", a=2, u=2),
+                in_=psv.rearrange("p a u t -> p a t u"),
             )
 
-        def bias_unit(s, h):
-            transpose_unit(b_sb[s][:, 4 * h : 4 * h + 4, :], bT[s][:, h * UNIT : h * UNIT + UNIT, :])
+        def fetch(h):
+            if h >= len(units):
+                return
+            s, b, q = units[h]
+            xg[h] = work.tile([P, HU, 4], BF16, name="xg", tag="xg", align_bytes=64)
+            transposed(x_sb[s][:, b, 2 * q : 2 * q + 2, :], xg[h][:])
+            if b == 0:
+                transposed(b_sb[s][:, 2 * q : 2 * q + 2, :], bT[s][:, HU * q : HU * q + HU, :])
 
-        def stage1_unit(s, b, h):
-            c0 = b * T + h * UNIT
-            pre = work.tile([P, UNIT, 4], BF16, name="pre", tag="pre", align_bytes=64)
-            for tt in range(4):
-                ps = psum.tile([P, 512], F32, name="s1", tag="bank")
-                psv = ps[:].rearrange("p (j t) -> p j t", j=4)
-                for j in range(4):
-                    nc.tensor.matmul_mx(
-                        out=psv[:, j, :],
-                        lhsT=w_codes[s][:, P * j : P * j + P].bitcast(FP8X4),
-                        lhsT_scale=w_scales[s][:, P * j : P * j + P],
-                        rhs=x_codes[s][:, c0 + P * tt : c0 + P * tt + P].bitcast(FP8X4),
-                        rhs_scale=x_scales[s][:, c0 + P * tt : c0 + P * tt + P],
-                        start=True,
-                        stop=True,
-                    )
-                nc.vector.tensor_tensor(
-                    out=pre[:, P * tt : P * tt + P, :],
-                    in0=psv.rearrange("p j t -> p t j"),
-                    in1=bT[s][:, h * UNIT + P * tt : h * UNIT + P * tt + P, :],
-                    op=ALU.add,
-                )
-            flat = pre[:].rearrange("p t j -> p (t j)")
-            nc.gpsimd.tensor_scalar(out=flat, in0=flat, scalar1=FMAX, scalar2=0.0, op0=ALU.min, op1=ALU.max)
+        def col0(h):
+            s, b, q = units[h]
+            return b * T + q * HU
+
+        def quantise_x(h):
+            if h >= len(units):
+                return
+            s = units[h][0]
+            c0 = col0(h)
             nc.vector.quantize_mx(
-                out=e_codes[s][:, c0 : c0 + UNIT].bitcast(FP8X4),
-                scales=e_scales[s][:, c0 : c0 + UNIT],
-                in_=flat,
+                out=x_codes[s][:, c0 : c0 + HU].bitcast(FP8X4),
+                scales=x_scales[s][:, c0 : c0 + HU],
+                in_=xg[h][:].rearrange("p t j -> p (t j)"),
             )
 
-        def stage2_tile(b, n):
-            i0 = b * T + P * n
-            banks = []
-            part = small.tile([P, 2], F32, name="part", tag="part")
+        def project(h, a):
+            if h >= len(units):
+                return
+            s = units[h][0]
+            c0 = col0(h) + P * a
+            s1[h, a] = psum.tile([P, 512], F32, name="s1", tag="s1")
+            psv = s1[h, a][:].rearrange("p (j t) -> p j t", j=4)
+            for j in range(4):
+                nc.tensor.matmul_mx(
+                    out=psv[:, j, :],
+                    lhsT=w_codes[s][:, P * j : P * j + P].bitcast(FP8X4),
+                    lhsT_scale=w_scales[s][:, P * j : P * j + P],
+                    rhs=x_codes[s][:, c0 : c0 + P].bitcast(FP8X4),
+                    rhs_scale=x_scales[s][:, c0 : c0 + P],
+                    start=True,
+                    stop=True,
+                )
+
+        def add_bias(h, a):
+            s, b, q = units[h]
+            if a == 0:
+                pre[h] = work.tile([P, HU, 4], BF16, name="pre", tag="pre", align_bytes=64)
+            nc.vector.tensor_tensor(
+                out=pre[h][:, P * a : P * a + P, :],
+                in0=s1[h, a][:].rearrange("p (j t) -> p t j", j=4),
+                in1=bT[s][:, HU * q + P * a : HU * q + P * a + P, :],
+                op=ALU.add,
+            )
+
+        def relu(h):
+            flat = pre[h][:].rearrange("p t j -> p (t j)")
+            nc.vector.tensor_scalar_max(out=flat, in0=flat, scalar1=0.0)
+
+        def quantise_e(h):
+            if h < 0:
+                return
+            s = units[h][0]
+            c0 = col0(h)
+            nc.vector.quantize_mx(
+                out=e_codes[s][:, c0 : c0 + HU].bitcast(FP8X4),
+                scales=e_scales[s][:, c0 : c0 + HU],
+                in_=pre[h][:].rearrange("p t j -> p (t j)"),
+            )
+
+        def scores(t):
+            b = t // 8
+            i0 = P * t
+            tag = {14: "tp", 15: "s1"}.get(t, "sc")
             for hh in range(2):
-                sc = psum.tile([P, 512], F32, name="sc", tag="bank")
+                sc[t, hh] = psum.tile([P, 512], F32, name="sc", tag=tag, bufs=4 if tag == "sc" else 2)
                 j0 = b * T + 512 * hh
                 nc.tensor.matmul_mx(
-                    out=sc[:],
+                    out=sc[t, hh][:],
                     lhsT=e_codes[2][:, i0 : i0 + P].bitcast(FP8X4),
                     lhsT_scale=e_scales[2][:, i0 : i0 + P],
                     rhs=e_codes[1][:, j0 : j0 + 512].bitcast(FP8X4),
@@ -161,74 +198,126 @@ def tile_attentionmm_pa_kernel(tc, x1, x2, W1, W2, b1, b2, out):
                     start=True,
                     stop=True,
                 )
-                nc.vector.tensor_reduce(out=part[:, hh : hh + 1], in_=sc[:], axis=AX.X, op=ALU.max)
-                banks.append(sc)
-            negm = small.tile([P, 1], F32, name="negm", tag="negm")
-            nc.vector.tensor_reduce(out=negm[:], in_=part[:], axis=AX.X, op=ALU.max, negate=True)
-            ex = expool.tile([P, T], F32, name="ex", tag="ex")
-            sums = small.tile([P, 2], F32, name="sums", tag="sums")
+
+        def bank_max(t, hh):
+            if hh == 0:
+                part[t] = small.tile([P, 2], F32, name="part", tag="part")
+            nc.vector.tensor_reduce(out=part[t][:, hh : hh + 1], in_=sc[t, hh][:], axis=AX.X, op=ALU.max)
+
+        def row_max(t):
+            negm[t] = small.tile([P, 1], F32, name="negm", tag="negm")
+            nc.vector.tensor_reduce(out=negm[t][:], in_=part[t][:], axis=AX.X, op=ALU.max, negate=True)
+
+        def exponent(t):
+            ex[t] = expool.tile([P, T], F32, name="ex", tag="ex")
+            sums[t] = small.tile([P, 2], F32, name="sums", tag="sums")
             for hh in range(2):
                 nc.scalar.activation(
-                    out=ex[:, 512 * hh : 512 * hh + 512],
-                    in_=banks[hh][:],
+                    out=ex[t][:, 512 * hh : 512 * hh + 512],
+                    in_=sc[t, hh][:],
                     func=ACT.Exp,
-                    bias=negm[:, 0:1],
+                    bias=negm[t][:, 0:1],
                     scale=1.0,
-                    accum_out=sums[:, hh : hh + 1],
+                    accum_out=sums[t][:, hh : hh + 1],
                 )
-            tot = small.tile([P, 1], F32, name="tot", tag="tot")
-            nc.vector.tensor_reduce(out=tot[:], in_=sums[:], axis=AX.X, op=ALU.add)
-            rs = small.tile([P, 1], F32, name="rs", tag="rs")
-            nc.vector.reciprocal(out=rs[:], in_=tot[:])
-            nc.gpsimd.tensor_scalar(out=ex[:], in0=ex[:], scalar1=rs[:, 0:1], scalar2=0.0, op0=ALU.mult, op1=ALU.add)
-            nc.sync.dma_start(out=out_view[:, b, n, :], in_=ex[:])
 
-        load_w(1)
-        load_x(1, 0, 0)
-        load_b(1, 0)
-        load_x(1, 0, 1)
-        load_b(1, 1)
-        load_w(2)
-        load_x(2, 0, 0)
-        load_b(2, 0)
-        load_x(2, 0, 1)
-        load_b(2, 1)
-        load_x(1, 1, 0)
-        load_x(1, 1, 1)
-        load_x(2, 1, 0)
-        load_x(2, 1, 1)
+        def row_sum(t):
+            tot[t] = small.tile([P, 1], F32, name="tot", tag="tot")
+            nc.vector.tensor_reduce(out=tot[t][:], in_=sums[t][:], axis=AX.X, op=ALU.add)
 
-        prep_w(1)
-        x_unit(1, 0, 0)
-        bias_unit(1, 0)
-        stage1_unit(1, 0, 0)
-        x_unit(1, 0, 1)
-        bias_unit(1, 1)
-        stage1_unit(1, 0, 1)
-        prep_w(2)
-        x_unit(2, 0, 0)
-        bias_unit(2, 0)
-        stage1_unit(2, 0, 0)
-        stage2_tile(0, 0)
-        stage2_tile(0, 1)
-        x_unit(2, 0, 1)
-        bias_unit(2, 1)
-        stage1_unit(2, 0, 1)
-        stage2_tile(0, 2)
-        stage2_tile(0, 3)
-        x_unit(1, 1, 0)
-        stage1_unit(1, 1, 0)
-        stage2_tile(0, 4)
-        stage2_tile(0, 5)
-        x_unit(1, 1, 1)
-        stage1_unit(1, 1, 1)
-        stage2_tile(0, 6)
-        stage2_tile(0, 7)
-        x_unit(2, 1, 0)
-        stage1_unit(2, 1, 0)
-        stage2_tile(1, 0)
-        stage2_tile(1, 1)
-        x_unit(2, 1, 1)
-        stage1_unit(2, 1, 1)
-        for n in range(2, 8):
-            stage2_tile(1, n)
+        def inverse(t):
+            rs[t] = small.tile([P, 1], F32, name="rs", tag="rs")
+            nc.vector.reciprocal(out=rs[t][:], in_=tot[t][:])
+
+        def normalise(t):
+            row = out_view[:, t // 8, t % 8, :]
+            if t == 15:
+                nc.vector.tensor_scalar_mul(out=ex[t][:, 0:512], in0=ex[t][:, 0:512], scalar1=rs[t][:, 0:1])
+                nc.sync.dma_start(out=row[:, 0:512], in_=ex[t][:, 0:512])
+                nc.scalar.activation(out=ex[t][:, 512:T], in_=ex[t][:, 512:T], func=ACT.Copy, scale=rs[t][:, 0:1])
+                nc.sync.dma_start(out=row[:, 512:T], in_=ex[t][:, 512:T])
+                return
+            if t in NORM_ON_VECTOR:
+                nc.vector.tensor_scalar_mul(out=ex[t][:], in0=ex[t][:], scalar1=rs[t][:, 0:1])
+            else:
+                nc.scalar.activation(out=ex[t][:], in_=ex[t][:], func=ACT.Copy, scale=rs[t][:, 0:1])
+            nc.sync.dma_start(out=row, in_=ex[t][:])
+
+        NORM_ON_VECTOR = (8, 9, 10, 11, 12, 13, 14)
+        tiles_of = {c: [c - 6] for c in range(6, 14)}
+        for c in range(14, 18):
+            tiles_of[c] = [2 * c - 20, 2 * c - 19]
+        finish_with = {t: t - 1 for t in range(1, 9)}
+        for t in range(9 + 1, 16):
+            finish_with[t] = t - 2
+
+        regroup_w(1, nc.vector.tensor_copy)
+        quantise_w(1)
+        fetch(0)
+        fetch(1)
+        quantise_x(0)
+        project(0, 0)
+        project(0, 1)
+        fetch(2)
+
+        for c in range(18):
+            now = tiles_of.get(c, [])
+            after = tiles_of.get(c + 1, [])
+            unit = c < len(units)
+            first = now[0] if now else None
+            done = finish_with.get(first)
+            if c >= 4:
+                fetch(c + 3)
+            if unit:
+                add_bias(c, 0)
+                quantise_x(c + 1)
+            if c == len(units):
+                quantise_e(c - 1)
+                for t in after:
+                    scores(t)
+            if now:
+                bank_max(first, 0)
+            if done is not None:
+                row_sum(done)
+            if unit:
+                project(c + 1, 0)
+                add_bias(c, 1)
+            if now:
+                bank_max(first, 1)
+            if unit:
+                project(c + 1, 1)
+                quantise_e(c - 1)
+            if done is not None:
+                inverse(done)
+            if now:
+                row_max(first)
+                exponent(first)
+            if unit:
+                relu(c)
+            if c == 1:
+                regroup_w(2, nc.scalar.copy)
+            if c == 2:
+                quantise_w(2)
+            if c < 4:
+                fetch(c + 3)
+            if done is not None:
+                normalise(done)
+            for t in now[1:]:
+                done = finish_with.get(t)
+                bank_max(t, 0)
+                if done is not None:
+                    row_sum(done)
+                bank_max(t, 1)
+                if done is not None:
+                    inverse(done)
+                row_max(t)
+                exponent(t)
+                if done is not None:
+                    normalise(done)
+            if unit:
+                for t in after:
+                    scores(t)
+        for t in (14, 15):
+            row_sum(t)
+            inverse(t)
+            normalise(t)

@@ -25,8 +25,8 @@ def tile_attentionmm_pa_kernel(tc, x1, x2, W1, W2, b1, b2, out):
         if PIN:
             ctx.enter_context(tc.manual_schedule())
         keep = ctx.enter_context(tc.tile_pool(name="keep", bufs=1))
-        work = ctx.enter_context(tc.tile_pool(name="work", bufs=4))
-        expool = ctx.enter_context(tc.tile_pool(name="expool", bufs=6))
+        work = ctx.enter_context(tc.tile_pool(name="work", bufs=5))
+        expool = ctx.enter_context(tc.tile_pool(name="expool", bufs=8))
         small = ctx.enter_context(tc.tile_pool(name="small", bufs=8))
         psum = ctx.enter_context(tc.psum_pool(name="psum", bufs=2))
 
@@ -88,12 +88,11 @@ def tile_attentionmm_pa_kernel(tc, x1, x2, W1, W2, b1, b2, out):
         units = [(s, b, q) for b in range(B) for s in (1, 2) for q in range(4)]
         xg, pre, s1, sc, part, negm, ex, sums, tot, rs = {}, {}, {}, {}, {}, {}, {}, {}, {}, {}
 
-        def regroup_w(s, copy):
-            for u in range(2):
-                copy(
-                    out=wg[s][:, 256 * u : 256 * u + 256, :].rearrange("q (e p) s -> q e p s", e=2),
-                    in_=w_sb[s][:, :, 256 * u : 256 * u + 256].rearrange("q s (p e) -> q e p s", e=2),
-                )
+        def regroup_w(s, u, copy):
+            copy(
+                out=wg[s][:, 256 * u : 256 * u + 256, :].rearrange("q (e p) s -> q e p s", e=2),
+                in_=w_sb[s][:, :, 256 * u : 256 * u + 256].rearrange("q s (p e) -> q e p s", e=2),
+            )
 
         def quantise_w(s):
             nc.vector.quantize_mx(
@@ -169,7 +168,12 @@ def tile_attentionmm_pa_kernel(tc, x1, x2, W1, W2, b1, b2, out):
 
         def relu(h):
             flat = pre[h][:].rearrange("p t j -> p (t j)")
-            nc.vector.tensor_scalar_max(out=flat, in0=flat, scalar1=0.0)
+            if h in RELU_ON_SCALAR:
+                nc.scalar.activation(out=flat, in_=flat, func=ACT.Relu)
+            else:
+                nc.vector.tensor_scalar_max(out=flat, in0=flat, scalar1=0.0)
+
+        RELU_ON_SCALAR = (6, 7, 8, 9, 10, 11, 12, 13)
 
         def quantise_e(h):
             if h < 0:
@@ -229,21 +233,37 @@ def tile_attentionmm_pa_kernel(tc, x1, x2, W1, W2, b1, b2, out):
             rs[t] = small.tile([P, 1], F32, name="rs", tag="rs")
             nc.vector.reciprocal(out=rs[t][:], in_=tot[t][:])
 
+        def scale_rows(engine, t, lo, hi):
+            part_ex = ex[t][:, lo:hi]
+            if engine == "gpsimd":
+                nc.gpsimd.tensor_scalar(
+                    out=part_ex, in0=part_ex, scalar1=rs[t][:, 0:1], scalar2=0.0, op0=ALU.mult, op1=ALU.add
+                )
+            elif engine == "vector":
+                nc.vector.tensor_scalar_mul(out=part_ex, in0=part_ex, scalar1=rs[t][:, 0:1])
+            else:
+                nc.scalar.activation(out=part_ex, in_=part_ex, func=ACT.Copy, scale=rs[t][:, 0:1])
+
         def normalise(t):
             row = out_view[:, t // 8, t % 8, :]
-            if t == 15:
-                nc.vector.tensor_scalar_mul(out=ex[t][:, 0:512], in0=ex[t][:, 0:512], scalar1=rs[t][:, 0:1])
-                nc.sync.dma_start(out=row[:, 0:512], in_=ex[t][:, 0:512])
-                nc.scalar.activation(out=ex[t][:, 512:T], in_=ex[t][:, 512:T], func=ACT.Copy, scale=rs[t][:, 0:1])
-                nc.sync.dma_start(out=row[:, 512:T], in_=ex[t][:, 512:T])
-                return
-            if t in NORM_ON_VECTOR:
-                nc.vector.tensor_scalar_mul(out=ex[t][:], in0=ex[t][:], scalar1=rs[t][:, 0:1])
+            first_half, second_half = NORMALISERS.get(t, ("scalar", "scalar"))
+            if first_half == second_half:
+                scale_rows(first_half, t, 0, T)
             else:
-                nc.scalar.activation(out=ex[t][:], in_=ex[t][:], func=ACT.Copy, scale=rs[t][:, 0:1])
-            nc.sync.dma_start(out=row, in_=ex[t][:])
+                scale_rows(first_half, t, 0, 512)
+                scale_rows(second_half, t, 512, T)
+            if t == 15:
+                nc.sync.dma_start(out=row[:, 0:512], in_=ex[t][:, 0:512])
+                nc.sync.dma_start(out=row[:, 512:T], in_=ex[t][:, 512:T])
+            else:
+                nc.sync.dma_start(out=row, in_=ex[t][:])
 
-        NORM_ON_VECTOR = (8, 9, 10, 11, 12, 13, 14)
+        def finish(t):
+            row_sum(t)
+            inverse(t)
+            normalise(t)
+
+        NORMALISERS = {0: ("gpsimd", "gpsimd"), 1: ("gpsimd", "gpsimd"), 2: ("gpsimd", "gpsimd"), 3: ("gpsimd", "gpsimd"), 4: ("gpsimd", "gpsimd"), 5: ("gpsimd", "gpsimd"), 6: ("gpsimd", "gpsimd"), 7: ("gpsimd", "gpsimd"), 8: ("gpsimd", "gpsimd"), 9: ("scalar", "scalar"), 10: ("gpsimd", "gpsimd"), 11: ("scalar", "scalar"), 12: ("gpsimd", "gpsimd"), 13: ("gpsimd", "gpsimd"), 14: ("gpsimd", "gpsimd"), 15: ("vector", "scalar")}
         tiles_of = {c: [c - 6] for c in range(6, 14)}
         for c in range(14, 18):
             tiles_of[c] = [2 * c - 20, 2 * c - 19]
@@ -251,7 +271,8 @@ def tile_attentionmm_pa_kernel(tc, x1, x2, W1, W2, b1, b2, out):
         for t in range(9 + 1, 16):
             finish_with[t] = t - 2
 
-        regroup_w(1, nc.vector.tensor_copy)
+        regroup_w(1, 0, nc.vector.tensor_copy)
+        regroup_w(1, 1, nc.vector.tensor_copy)
         quantise_w(1)
         fetch(0)
         fetch(1)
@@ -262,62 +283,47 @@ def tile_attentionmm_pa_kernel(tc, x1, x2, W1, W2, b1, b2, out):
 
         for c in range(18):
             now = tiles_of.get(c, [])
-            after = tiles_of.get(c + 1, [])
             unit = c < len(units)
-            first = now[0] if now else None
-            done = finish_with.get(first)
-            if c >= 4:
-                fetch(c + 3)
-            if unit:
-                add_bias(c, 0)
-                quantise_x(c + 1)
-            if c == len(units):
-                quantise_e(c - 1)
-                for t in after:
-                    scores(t)
-            if now:
-                bank_max(first, 0)
-            if done is not None:
-                row_sum(done)
-            if unit:
-                project(c + 1, 0)
-                add_bias(c, 1)
-            if now:
-                bank_max(first, 1)
-            if unit:
-                project(c + 1, 1)
-                quantise_e(c - 1)
-            if done is not None:
-                inverse(done)
-            if now:
-                row_max(first)
-                exponent(first)
-            if unit:
+            for a in range(2):
+                if unit:
+                    add_bias(c, a)
+                    if c == 0 and a == 0:
+                        quantise_x(1)
+                    project(c + 1, a)
+                if now:
+                    bank_max(now[0], a)
+            if unit and c in RELU_ON_SCALAR:
                 relu(c)
-            if c == 1:
-                regroup_w(2, nc.scalar.copy)
-            if c == 2:
-                quantise_w(2)
-            if c < 4:
-                fetch(c + 3)
-            if done is not None:
-                normalise(done)
+            if now:
+                row_max(now[0])
+                exponent(now[0])
+            if not unit:
+                finish(now[0] - 1)
             for t in now[1:]:
-                done = finish_with.get(t)
                 bank_max(t, 0)
-                if done is not None:
-                    row_sum(done)
                 bank_max(t, 1)
-                if done is not None:
-                    inverse(done)
                 row_max(t)
                 exponent(t)
-                if done is not None:
-                    normalise(done)
+            if not unit:
+                finish(now[1] - 1)
+            if unit and c not in RELU_ON_SCALAR:
+                relu(c)
+            quantise_x(c + 2)
             if unit:
-                for t in after:
-                    scores(t)
-        for t in (14, 15):
-            row_sum(t)
-            inverse(t)
-            normalise(t)
+                quantise_e(c - 1)
+            if c == len(units) - 1:
+                quantise_e(c)
+            if c == 1:
+                regroup_w(2, 1, nc.vector.tensor_copy)
+            if c == 2:
+                quantise_w(2)
+            if unit and now:
+                for t in range(now[0] - 1, now[-1]):
+                    if t >= 0:
+                        finish(t)
+            if c == 1:
+                regroup_w(2, 0, nc.scalar.copy)
+            fetch(c + 3)
+            for t in tiles_of.get(c + 1, []):
+                scores(t)
+        finish(15)

@@ -263,7 +263,7 @@ def tile_attentionmm_pa_kernel(tc, x1, x2, W1, W2, b1, b2, out):
             inverse(t)
             normalise(t)
 
-        NORMALISERS = {0: ("gpsimd", "gpsimd"), 1: ("gpsimd", "gpsimd"), 2: ("gpsimd", "gpsimd"), 3: ("gpsimd", "gpsimd"), 4: ("gpsimd", "gpsimd"), 5: ("gpsimd", "gpsimd"), 6: ("gpsimd", "gpsimd"), 7: ("gpsimd", "gpsimd"), 8: ("gpsimd", "gpsimd"), 9: ("scalar", "scalar"), 10: ("gpsimd", "gpsimd"), 11: ("scalar", "scalar"), 12: ("gpsimd", "gpsimd"), 13: ("gpsimd", "gpsimd"), 14: ("gpsimd", "gpsimd"), 15: ("vector", "scalar")}
+        NORMALISERS = {0: ("gpsimd", "gpsimd"), 1: ("gpsimd", "gpsimd"), 2: ("gpsimd", "gpsimd"), 3: ("gpsimd", "gpsimd"), 4: ("gpsimd", "gpsimd"), 5: ("gpsimd", "gpsimd"), 6: ("gpsimd", "gpsimd"), 7: ("gpsimd", "gpsimd"), 8: ("gpsimd", "gpsimd"), 9: ("gpsimd", "gpsimd"), 10: ("gpsimd", "gpsimd"), 11: ("gpsimd", "gpsimd"), 12: ("gpsimd", "gpsimd"), 13: ("vector", "vector"), 14: ("vector", "scalar"), 15: ("vector", "scalar")}
         tiles_of = {c: [c - 6] for c in range(6, 14)}
         for c in range(14, 18):
             tiles_of[c] = [2 * c - 20, 2 * c - 19]
@@ -281,49 +281,77 @@ def tile_attentionmm_pa_kernel(tc, x1, x2, W1, W2, b1, b2, out):
         project(0, 1)
         fetch(2)
 
-        for c in range(18):
+        for c in range(16):
             now = tiles_of.get(c, [])
-            unit = c < len(units)
-            for a in range(2):
-                if unit:
-                    add_bias(c, a)
-                    if c == 0 and a == 0:
-                        quantise_x(1)
-                    project(c + 1, a)
-                if now:
-                    bank_max(now[0], a)
-            if unit and c in RELU_ON_SCALAR:
+            two = len(now) == 2
+            fin = [t for t in range(now[0] - 1, now[-1]) if t >= 0] if now else []
+            add_bias(c, 0)
+            if c == 0:
+                quantise_x(1)
+            project(c + 1, 0)
+            if now:
+                bank_max(now[0], 0)
+            add_bias(c, 1)
+            project(c + 1, 1)
+            if now:
+                bank_max(now[0], 1)
+            else:
+                quantise_x(c + 2)
+            if c in RELU_ON_SCALAR:
+                relu(c)
+            if two:
+                bank_max(now[1], 0)
+            if c in RELU_ON_SCALAR:
+                quantise_x(c + 2)
+            else:
                 relu(c)
             if now:
                 row_max(now[0])
                 exponent(now[0])
-            if not unit:
-                finish(now[0] - 1)
-            for t in now[1:]:
-                bank_max(t, 0)
-                bank_max(t, 1)
-                row_max(t)
-                exponent(t)
-            if not unit:
-                finish(now[1] - 1)
-            if unit and c not in RELU_ON_SCALAR:
-                relu(c)
-            quantise_x(c + 2)
-            if unit:
-                quantise_e(c - 1)
-            if c == len(units) - 1:
-                quantise_e(c)
+                if c not in RELU_ON_SCALAR:
+                    quantise_x(c + 2)
+            if two:
+                bank_max(now[1], 1)
+            if fin:
+                row_sum(fin[0])
+            quantise_e(c - 1)
+            if two:
+                row_max(now[1])
+                exponent(now[1])
+                row_sum(fin[1])
             if c == 1:
                 regroup_w(2, 1, nc.vector.tensor_copy)
             if c == 2:
                 quantise_w(2)
-            if unit and now:
-                for t in range(now[0] - 1, now[-1]):
-                    if t >= 0:
-                        finish(t)
+            if c == 15:
+                quantise_e(c)
+            for t in fin:
+                inverse(t)
+            for t in fin:
+                normalise(t)
             if c == 1:
                 regroup_w(2, 0, nc.scalar.copy)
             fetch(c + 3)
             for t in tiles_of.get(c + 1, []):
                 scores(t)
-        finish(15)
+        scores(14)
+        scores(15)
+        bank_max(12, 0)
+        bank_max(12, 1)
+        for t in range(13, 16):
+            bank_max(t, 0)
+            row_max(t - 1)
+            exponent(t - 1)
+            if t > 13:
+                inverse(t - 3)
+                normalise(t - 3)
+            bank_max(t, 1)
+            row_sum(t - 2)
+        row_max(15)
+        exponent(15)
+        inverse(13)
+        normalise(13)
+        for t in (14, 15):
+            row_sum(t)
+            inverse(t)
+            normalise(t)

@@ -62,14 +62,23 @@ def tile_attentionmm_pa_kernel(tc, x1, x2, W1, W2, b1, b2, out):
                 in_=ws[s].rearrange("(u q e) c -> q u e c", u=2, e=2),
             )
 
+        def load_w_columns(s, half):
+            cols = slice(256 * half, 256 * half + 256)
+            rows = ws[s].rearrange("(u q e) c -> q u e c", u=2, e=2)
+            for u in range(2):
+                nc.sync.dma_start(out=w_sb[s][:, 2 * u : 2 * u + 2, cols], in_=rows[:, u, :, cols])
+
         def load_x(s, b, n0, n1):
             nc.sync.dma_start(out=x_sb[s][:, b, n0:n1, :], in_=x_view[s][:, b, n0:n1, :])
 
         def load_b(s, n0, n1):
             nc.sync.dma_start(out=b_sb[s][:, n0:n1, :], in_=b_view[s][:, n0:n1, :])
 
-        load_w(1)
-        for q in range(4):
+        load_w_columns(1, 0)
+        load_x(1, 0, 0, 2)
+        load_w_columns(1, 1)
+        load_b(1, 0, 2)
+        for q in range(1, 4):
             load_x(1, 0, 2 * q, 2 * q + 2)
             load_b(1, 2 * q, 2 * q + 2)
         load_w(2)
@@ -94,11 +103,11 @@ def tile_attentionmm_pa_kernel(tc, x1, x2, W1, W2, b1, b2, out):
                 in_=w_sb[s][:, :, 256 * u : 256 * u + 256].rearrange("q s (p e) -> q e p s", e=2),
             )
 
-        def quantise_w(s):
+        def quantise_w(s, lo, hi):
             nc.vector.quantize_mx(
-                out=w_codes[s][:].bitcast(FP8X4),
-                scales=w_scales[s][:],
-                in_=wg[s][:].rearrange("q f s -> q (f s)"),
+                out=w_codes[s][:, lo:hi].bitcast(FP8X4),
+                scales=w_scales[s][:, lo:hi],
+                in_=wg[s][:, lo:hi, :].rearrange("q f s -> q (f s)"),
             )
 
         def transposed(src, dst):
@@ -173,7 +182,7 @@ def tile_attentionmm_pa_kernel(tc, x1, x2, W1, W2, b1, b2, out):
             else:
                 nc.vector.tensor_scalar_max(out=flat, in0=flat, scalar1=0.0)
 
-        RELU_ON_SCALAR = (6, 7, 8, 9, 10, 11, 12, 13)
+        RELU_ON_SCALAR = (3, 5, 6, 7, 8, 9, 10, 11, 12, 13, 14, 15)
 
         def quantise_e(h):
             if h < 0:
@@ -271,12 +280,13 @@ def tile_attentionmm_pa_kernel(tc, x1, x2, W1, W2, b1, b2, out):
         for t in range(9 + 1, 16):
             finish_with[t] = t - 2
 
+        fetch(0)
         regroup_w(1, 0, nc.vector.tensor_copy)
         regroup_w(1, 1, nc.vector.tensor_copy)
-        quantise_w(1)
-        fetch(0)
-        fetch(1)
+        quantise_w(1, 0, 256)
         quantise_x(0)
+        quantise_w(1, 256, E)
+        fetch(1)
         project(0, 0)
         project(0, 1)
         fetch(2)
@@ -293,22 +303,21 @@ def tile_attentionmm_pa_kernel(tc, x1, x2, W1, W2, b1, b2, out):
                 bank_max(now[0], 0)
             add_bias(c, 1)
             project(c + 1, 1)
+            on_scalar = c in RELU_ON_SCALAR
+            if on_scalar:
+                relu(c)
             if now:
                 bank_max(now[0], 1)
-            else:
-                quantise_x(c + 2)
-            if c in RELU_ON_SCALAR:
-                relu(c)
             if two:
                 bank_max(now[1], 0)
-            if c in RELU_ON_SCALAR:
+            if on_scalar or not now:
                 quantise_x(c + 2)
-            else:
+            if not on_scalar:
                 relu(c)
             if now:
                 row_max(now[0])
                 exponent(now[0])
-                if c not in RELU_ON_SCALAR:
+                if not on_scalar:
                     quantise_x(c + 2)
             if two:
                 bank_max(now[1], 1)
@@ -322,7 +331,7 @@ def tile_attentionmm_pa_kernel(tc, x1, x2, W1, W2, b1, b2, out):
             if c == 1:
                 regroup_w(2, 1, nc.vector.tensor_copy)
             if c == 2:
-                quantise_w(2)
+                quantise_w(2, 0, E)
             if c == 15:
                 quantise_e(c)
             for t in fin:
@@ -331,7 +340,13 @@ def tile_attentionmm_pa_kernel(tc, x1, x2, W1, W2, b1, b2, out):
                 normalise(t)
             if c == 1:
                 regroup_w(2, 0, nc.scalar.copy)
-            fetch(c + 3)
+            if c < 5:
+                fetch(c + 3)
+            elif c == 5:
+                fetch(c + 3)
+                fetch(c + 4)
+            else:
+                fetch(c + 4)
             for t in tiles_of.get(c + 1, []):
                 scores(t)
         scores(14)

@@ -14,16 +14,20 @@ AX = mybir.AxisListType
 
 B, T, E = 2, 1024, 512
 P = 128
-HU = 256
+BANK = 512
+SLAB = 256
+N_SLABS = 2 * B * T // SLAB
+N_ROW_TILES = B * T // P
 FLOPS = 2 * (2 * B * T * E * E) + 2 * B * T * T * E
-PIN = True
+
+SCALAR_RELU_FROM = 5
+VECTOR_SCALES_FROM = 12
 
 
 def tile_attentionmm_pa_kernel(tc, x1, x2, W1, W2, b1, b2, out):
     nc = tc.nc
     with ExitStack() as ctx:
-        if PIN:
-            ctx.enter_context(tc.manual_schedule())
+        ctx.enter_context(tc.manual_schedule())
         keep = ctx.enter_context(tc.tile_pool(name="keep", bufs=1))
         work = ctx.enter_context(tc.tile_pool(name="work", bufs=5))
         expool = ctx.enter_context(tc.tile_pool(name="expool", bufs=8))
@@ -62,29 +66,20 @@ def tile_attentionmm_pa_kernel(tc, x1, x2, W1, W2, b1, b2, out):
                 in_=ws[s].rearrange("(u q e) c -> q u e c", u=2, e=2),
             )
 
-        def load_w_columns(s, half):
-            cols = slice(256 * half, 256 * half + 256)
-            rows = ws[s].rearrange("(u q e) c -> q u e c", u=2, e=2)
-            for u in range(2):
-                nc.sync.dma_start(out=w_sb[s][:, 2 * u : 2 * u + 2, cols], in_=rows[:, u, :, cols])
-
         def load_x(s, b, n0, n1):
             nc.sync.dma_start(out=x_sb[s][:, b, n0:n1, :], in_=x_view[s][:, b, n0:n1, :])
 
         def load_b(s, n0, n1):
             nc.sync.dma_start(out=b_sb[s][:, n0:n1, :], in_=b_view[s][:, n0:n1, :])
 
-        load_w_columns(1, 0)
-        load_x(1, 0, 0, 2)
-        load_w_columns(1, 1)
-        load_b(1, 0, 2)
-        for q in range(1, 4):
+        load_w(1)
+        for q in range(4):
             load_x(1, 0, 2 * q, 2 * q + 2)
             load_b(1, 2 * q, 2 * q + 2)
         load_w(2)
-        for h in range(2):
-            load_x(2, 0, 4 * h, 4 * h + 4)
-            load_b(2, 4 * h, 4 * h + 4)
+        for half in range(2):
+            load_x(2, 0, 4 * half, 4 * half + 4)
+            load_b(2, 4 * half, 4 * half + 4)
         load_x(1, 1, 0, 8)
         load_x(2, 1, 0, 8)
 
@@ -94,7 +89,7 @@ def tile_attentionmm_pa_kernel(tc, x1, x2, W1, W2, b1, b2, out):
         nc.vector.memset(warm[:], 0.0)
         nc.scalar.activation(out=warm[:], in_=warm[:], func=ACT.Exp)
 
-        units = [(s, b, q) for b in range(B) for s in (1, 2) for q in range(4)]
+        slabs = [(s, b, q) for b in range(B) for s in (1, 2) for q in range(4)]
         xg, pre, s1, sc, part, negm, ex, sums, tot, rs = {}, {}, {}, {}, {}, {}, {}, {}, {}, {}
 
         def regroup_w(s, u, copy):
@@ -103,59 +98,57 @@ def tile_attentionmm_pa_kernel(tc, x1, x2, W1, W2, b1, b2, out):
                 in_=w_sb[s][:, :, 256 * u : 256 * u + 256].rearrange("q s (p e) -> q e p s", e=2),
             )
 
-        def quantise_w(s, lo, hi):
+        def quantise_w(s):
             nc.vector.quantize_mx(
-                out=w_codes[s][:, lo:hi].bitcast(FP8X4),
-                scales=w_scales[s][:, lo:hi],
-                in_=wg[s][:, lo:hi, :].rearrange("q f s -> q (f s)"),
+                out=w_codes[s][:].bitcast(FP8X4),
+                scales=w_scales[s][:],
+                in_=wg[s][:].rearrange("q f s -> q (f s)"),
             )
 
-        def transposed(src, dst):
-            ps = psum.tile([P, 512], F32, name="tp", tag="tp")
-            psv = ps[:].rearrange("p (a u t) -> p a u t", a=2, u=2)
+        def transpose_pair(src, dst):
+            bank = psum.tile([P, BANK], F32, name="tp", tag="tp")
+            planes = bank[:].rearrange("p (a u t) -> p a u t", a=2, u=2)
             for a in range(2):
                 words = src[:, a, :].bitcast(F32)
                 for u in range(2):
-                    nc.tensor.transpose(psv[:, a, u, :], words[:, P * u : P * u + P], ident[:])
+                    nc.tensor.transpose(planes[:, a, u, :], words[:, P * u : P * u + P], ident[:])
             nc.scalar.copy(
                 out=dst.rearrange("p t j -> p (t j)").bitcast(F32).rearrange("p (a t u) -> p a t u", a=2, u=2),
-                in_=psv.rearrange("p a u t -> p a t u"),
+                in_=planes.rearrange("p a u t -> p a t u"),
             )
 
-        def fetch(h):
-            if h >= len(units):
-                return
-            s, b, q = units[h]
-            xg[h] = work.tile([P, HU, 4], BF16, name="xg", tag="xg", align_bytes=64)
-            transposed(x_sb[s][:, b, 2 * q : 2 * q + 2, :], xg[h][:])
+        def transpose_slab(h):
+            s, b, q = slabs[h]
+            xg[h] = work.tile([P, SLAB, 4], BF16, name="xg", tag="xg", align_bytes=64)
+            transpose_pair(x_sb[s][:, b, 2 * q : 2 * q + 2, :], xg[h][:])
             if b == 0:
-                transposed(b_sb[s][:, 2 * q : 2 * q + 2, :], bT[s][:, HU * q : HU * q + HU, :])
+                transpose_pair(b_sb[s][:, 2 * q : 2 * q + 2, :], bT[s][:, SLAB * q : SLAB * q + SLAB, :])
 
-        def col0(h):
-            s, b, q = units[h]
-            return b * T + q * HU
+        def first_column(h):
+            s, b, q = slabs[h]
+            return b * T + q * SLAB
 
         def quantise_x(h):
-            if h >= len(units):
+            if h >= N_SLABS:
                 return
-            s = units[h][0]
-            c0 = col0(h)
+            s = slabs[h][0]
+            c0 = first_column(h)
             nc.vector.quantize_mx(
-                out=x_codes[s][:, c0 : c0 + HU].bitcast(FP8X4),
-                scales=x_scales[s][:, c0 : c0 + HU],
+                out=x_codes[s][:, c0 : c0 + SLAB].bitcast(FP8X4),
+                scales=x_scales[s][:, c0 : c0 + SLAB],
                 in_=xg[h][:].rearrange("p t j -> p (t j)"),
             )
 
         def project(h, a):
-            if h >= len(units):
+            if h >= N_SLABS:
                 return
-            s = units[h][0]
-            c0 = col0(h) + P * a
-            s1[h, a] = psum.tile([P, 512], F32, name="s1", tag="s1")
-            psv = s1[h, a][:].rearrange("p (j t) -> p j t", j=4)
+            s = slabs[h][0]
+            c0 = first_column(h) + P * a
+            s1[h, a] = psum.tile([P, BANK], F32, name="s1", tag="s1")
+            by_j = s1[h, a][:].rearrange("p (j t) -> p j t", j=4)
             for j in range(4):
                 nc.tensor.matmul_mx(
-                    out=psv[:, j, :],
+                    out=by_j[:, j, :],
                     lhsT=w_codes[s][:, P * j : P * j + P].bitcast(FP8X4),
                     lhsT_scale=w_scales[s][:, P * j : P * j + P],
                     rhs=x_codes[s][:, c0 : c0 + P].bitcast(FP8X4),
@@ -165,49 +158,45 @@ def tile_attentionmm_pa_kernel(tc, x1, x2, W1, W2, b1, b2, out):
                 )
 
         def add_bias(h, a):
-            s, b, q = units[h]
+            s, b, q = slabs[h]
             if a == 0:
-                pre[h] = work.tile([P, HU, 4], BF16, name="pre", tag="pre", align_bytes=64)
+                pre[h] = work.tile([P, SLAB, 4], BF16, name="pre", tag="pre", align_bytes=64)
             nc.vector.tensor_tensor(
                 out=pre[h][:, P * a : P * a + P, :],
                 in0=s1[h, a][:].rearrange("p (j t) -> p t j", j=4),
-                in1=bT[s][:, HU * q + P * a : HU * q + P * a + P, :],
+                in1=bT[s][:, SLAB * q + P * a : SLAB * q + P * a + P, :],
                 op=ALU.add,
             )
 
         def relu(h):
             flat = pre[h][:].rearrange("p t j -> p (t j)")
-            if h in RELU_ON_SCALAR:
+            if h >= SCALAR_RELU_FROM:
                 nc.scalar.activation(out=flat, in_=flat, func=ACT.Relu)
             else:
                 nc.vector.tensor_scalar_max(out=flat, in0=flat, scalar1=0.0)
 
-        RELU_ON_SCALAR = (3, 5, 6, 7, 8, 9, 10, 11, 12, 13, 14, 15)
-
         def quantise_e(h):
             if h < 0:
                 return
-            s = units[h][0]
-            c0 = col0(h)
+            s = slabs[h][0]
+            c0 = first_column(h)
             nc.vector.quantize_mx(
-                out=e_codes[s][:, c0 : c0 + HU].bitcast(FP8X4),
-                scales=e_scales[s][:, c0 : c0 + HU],
+                out=e_codes[s][:, c0 : c0 + SLAB].bitcast(FP8X4),
+                scales=e_scales[s][:, c0 : c0 + SLAB],
                 in_=pre[h][:].rearrange("p t j -> p (t j)"),
             )
 
         def scores(t):
-            b = t // 8
-            i0 = P * t
-            tag = {14: "tp", 15: "s1"}.get(t, "sc")
+            tag = {N_ROW_TILES - 2: "tp", N_ROW_TILES - 1: "s1"}.get(t, "sc")
             for hh in range(2):
-                sc[t, hh] = psum.tile([P, 512], F32, name="sc", tag=tag, bufs=4 if tag == "sc" else 2)
-                j0 = b * T + 512 * hh
+                sc[t, hh] = psum.tile([P, BANK], F32, name="sc", tag=tag, bufs=4 if tag == "sc" else 2)
+                j0 = (t // 8) * T + BANK * hh
                 nc.tensor.matmul_mx(
                     out=sc[t, hh][:],
-                    lhsT=e_codes[2][:, i0 : i0 + P].bitcast(FP8X4),
-                    lhsT_scale=e_scales[2][:, i0 : i0 + P],
-                    rhs=e_codes[1][:, j0 : j0 + 512].bitcast(FP8X4),
-                    rhs_scale=e_scales[1][:, j0 : j0 + 512],
+                    lhsT=e_codes[2][:, P * t : P * t + P].bitcast(FP8X4),
+                    lhsT_scale=e_scales[2][:, P * t : P * t + P],
+                    rhs=e_codes[1][:, j0 : j0 + BANK].bitcast(FP8X4),
+                    rhs_scale=e_scales[1][:, j0 : j0 + BANK],
                     start=True,
                     stop=True,
                 )
@@ -226,7 +215,7 @@ def tile_attentionmm_pa_kernel(tc, x1, x2, W1, W2, b1, b2, out):
             sums[t] = small.tile([P, 2], F32, name="sums", tag="sums")
             for hh in range(2):
                 nc.scalar.activation(
-                    out=ex[t][:, 512 * hh : 512 * hh + 512],
+                    out=ex[t][:, BANK * hh : BANK * hh + BANK],
                     in_=sc[t, hh][:],
                     func=ACT.Exp,
                     bias=negm[t][:, 0:1],
@@ -242,131 +231,118 @@ def tile_attentionmm_pa_kernel(tc, x1, x2, W1, W2, b1, b2, out):
             rs[t] = small.tile([P, 1], F32, name="rs", tag="rs")
             nc.vector.reciprocal(out=rs[t][:], in_=tot[t][:])
 
-        def scale_rows(engine, t, lo, hi):
-            part_ex = ex[t][:, lo:hi]
-            if engine == "gpsimd":
+        def scale_and_store(t):
+            if t >= VECTOR_SCALES_FROM:
+                nc.vector.tensor_scalar_mul(out=ex[t][:], in0=ex[t][:], scalar1=rs[t][:, 0:1])
+            else:
                 nc.gpsimd.tensor_scalar(
-                    out=part_ex, in0=part_ex, scalar1=rs[t][:, 0:1], scalar2=0.0, op0=ALU.mult, op1=ALU.add
+                    out=ex[t][:], in0=ex[t][:], scalar1=rs[t][:, 0:1], scalar2=0.0, op0=ALU.mult, op1=ALU.add
                 )
-            elif engine == "vector":
-                nc.vector.tensor_scalar_mul(out=part_ex, in0=part_ex, scalar1=rs[t][:, 0:1])
-            else:
-                nc.scalar.activation(out=part_ex, in_=part_ex, func=ACT.Copy, scale=rs[t][:, 0:1])
+            nc.sync.dma_start(out=out_view[:, t // 8, t % 8, :], in_=ex[t][:])
 
-        def normalise(t):
-            row = out_view[:, t // 8, t % 8, :]
-            first_half, second_half = NORMALISERS.get(t, ("scalar", "scalar"))
-            if first_half == second_half:
-                scale_rows(first_half, t, 0, T)
-            else:
-                scale_rows(first_half, t, 0, 512)
-                scale_rows(second_half, t, 512, T)
-            if t == 15:
-                nc.sync.dma_start(out=row[:, 0:512], in_=ex[t][:, 0:512])
-                nc.sync.dma_start(out=row[:, 512:T], in_=ex[t][:, 512:T])
-            else:
-                nc.sync.dma_start(out=row, in_=ex[t][:])
+        def row_tiles_of(c):
+            if c < 6:
+                return []
+            if c < 14:
+                return [c - 6]
+            return [2 * c - 20, 2 * c - 19]
 
-        def finish(t):
-            row_sum(t)
-            inverse(t)
-            normalise(t)
+        def last_slab_of(t):
+            return 8 * (t // 8) + 4 + (t % 8) // 2
 
-        NORMALISERS = {0: ("gpsimd", "gpsimd"), 1: ("gpsimd", "gpsimd"), 2: ("gpsimd", "gpsimd"), 3: ("gpsimd", "gpsimd"), 4: ("gpsimd", "gpsimd"), 5: ("gpsimd", "gpsimd"), 6: ("gpsimd", "gpsimd"), 7: ("gpsimd", "gpsimd"), 8: ("gpsimd", "gpsimd"), 9: ("gpsimd", "gpsimd"), 10: ("gpsimd", "gpsimd"), 11: ("gpsimd", "gpsimd"), 12: ("gpsimd", "gpsimd"), 13: ("vector", "vector"), 14: ("vector", "scalar"), 15: ("vector", "scalar")}
-        tiles_of = {c: [c - 6] for c in range(6, 14)}
-        for c in range(14, 18):
-            tiles_of[c] = [2 * c - 20, 2 * c - 19]
-        finish_with = {t: t - 1 for t in range(1, 9)}
-        for t in range(9 + 1, 16):
-            finish_with[t] = t - 2
-
-        fetch(0)
         regroup_w(1, 0, nc.vector.tensor_copy)
         regroup_w(1, 1, nc.vector.tensor_copy)
-        quantise_w(1, 0, 256)
+        quantise_w(1)
+        transpose_slab(0)
+        transpose_slab(1)
         quantise_x(0)
-        quantise_w(1, 256, E)
-        fetch(1)
         project(0, 0)
         project(0, 1)
-        fetch(2)
+        transpose_slab(2)
+        transposed = 3
 
-        for c in range(16):
-            now = tiles_of.get(c, [])
-            two = len(now) == 2
-            fin = [t for t in range(now[0] - 1, now[-1]) if t >= 0] if now else []
+        for c in range(N_SLABS):
+            tiles = row_tiles_of(c)
+            two = len(tiles) == 2
+            done = [t for t in range(tiles[0] - 1, tiles[-1]) if t >= 0] if tiles else []
+            fresh = bool(tiles) and last_slab_of(tiles[0]) == c - 2
+
             add_bias(c, 0)
             if c == 0:
                 quantise_x(1)
             project(c + 1, 0)
-            if now:
-                bank_max(now[0], 0)
+            if tiles and not fresh:
+                bank_max(tiles[0], 0)
             add_bias(c, 1)
             project(c + 1, 1)
-            on_scalar = c in RELU_ON_SCALAR
-            if on_scalar:
+            if fresh:
+                bank_max(tiles[0], 0)
+            if c >= SCALAR_RELU_FROM:
                 relu(c)
-            if now:
-                bank_max(now[0], 1)
+            if tiles:
+                bank_max(tiles[0], 1)
             if two:
-                bank_max(now[1], 0)
-            if on_scalar or not now:
-                quantise_x(c + 2)
-            if not on_scalar:
+                bank_max(tiles[1], 0)
+
+            quantise_x(c + 2)
+            if c < SCALAR_RELU_FROM:
                 relu(c)
-            if now:
-                row_max(now[0])
-                exponent(now[0])
-                if not on_scalar:
-                    quantise_x(c + 2)
+            if tiles:
+                row_max(tiles[0])
+                exponent(tiles[0])
             if two:
-                bank_max(now[1], 1)
-            if fin:
-                row_sum(fin[0])
+                bank_max(tiles[1], 1)
+            if done:
+                row_sum(done[0])
             quantise_e(c - 1)
             if two:
-                row_max(now[1])
-                exponent(now[1])
-                row_sum(fin[1])
+                row_max(tiles[1])
+                exponent(tiles[1])
+                row_sum(done[1])
             if c == 1:
                 regroup_w(2, 1, nc.vector.tensor_copy)
             if c == 2:
-                quantise_w(2, 0, E)
-            if c == 15:
+                quantise_w(2)
+            if c == N_SLABS - 1:
                 quantise_e(c)
-            for t in fin:
+            for t in done:
                 inverse(t)
-            for t in fin:
-                normalise(t)
+            for t in done:
+                scale_and_store(t)
             if c == 1:
                 regroup_w(2, 0, nc.scalar.copy)
-            if c < 5:
-                fetch(c + 3)
-            elif c == 5:
-                fetch(c + 3)
-                fetch(c + 4)
-            else:
-                fetch(c + 4)
-            for t in tiles_of.get(c + 1, []):
+
+            ahead = 3 if c < 5 else 4
+            while transposed < min(N_SLABS, c + ahead + 1):
+                transpose_slab(transposed)
+                transposed += 1
+            for t in row_tiles_of(c + 1):
                 scores(t)
+
         scores(14)
         scores(15)
         bank_max(12, 0)
         bank_max(12, 1)
-        for t in range(13, 16):
+        row_sum(11)
+        row_max(12)
+        exponent(12)
+        inverse(11)
+        scale_and_store(11)
+        bank_max(13, 0)
+        bank_max(13, 1)
+        for t in (14, 15):
             bank_max(t, 0)
             row_max(t - 1)
             exponent(t - 1)
-            if t > 13:
-                inverse(t - 3)
-                normalise(t - 3)
             bank_max(t, 1)
             row_sum(t - 2)
         row_max(15)
         exponent(15)
-        inverse(13)
-        normalise(13)
+        for t in (12, 13):
+            inverse(t)
+        for t in (12, 13):
+            scale_and_store(t)
         for t in (14, 15):
             row_sum(t)
             inverse(t)
-            normalise(t)
+            scale_and_store(t)

@@ -60,11 +60,10 @@ def tile_attentionmm_pa_kernel(tc, x1, x2, W1, W2, b1, b2, out):
             e_codes[s] = keep.tile([P, B * T], U32, name="e_codes%d" % s, align_bytes=64)
             e_scales[s] = keep.tile([P, B * T], U8, name="e_scales%d" % s, align_bytes=64)
 
-        def load_w(s):
-            nc.sync.dma_start(
-                out=w_sb[s][:].rearrange("q (u e) c -> q u e c", u=2),
-                in_=ws[s].rearrange("(u q e) c -> q u e c", u=2, e=2),
-            )
+        def load_w(s, c0, c1):
+            rows = ws[s].rearrange("(u q e) c -> q u e c", u=2, e=2)
+            for u in range(2):
+                nc.sync.dma_start(out=w_sb[s][:, 2 * u : 2 * u + 2, c0:c1], in_=rows[:, u, :, c0:c1])
 
         def load_x(s, b, n0, n1):
             nc.sync.dma_start(out=x_sb[s][:, b, n0:n1, :], in_=x_view[s][:, b, n0:n1, :])
@@ -72,11 +71,14 @@ def tile_attentionmm_pa_kernel(tc, x1, x2, W1, W2, b1, b2, out):
         def load_b(s, n0, n1):
             nc.sync.dma_start(out=b_sb[s][:, n0:n1, :], in_=b_view[s][:, n0:n1, :])
 
-        load_w(1)
-        for q in range(4):
+        load_w(1, 0, E // 2)
+        load_x(1, 0, 0, 2)
+        load_w(1, E // 2, E)
+        load_b(1, 0, 2)
+        for q in range(1, 4):
             load_x(1, 0, 2 * q, 2 * q + 2)
             load_b(1, 2 * q, 2 * q + 2)
-        load_w(2)
+        load_w(2, 0, E)
         for half in range(2):
             load_x(2, 0, 4 * half, 4 * half + 4)
             load_b(2, 4 * half, 4 * half + 4)
@@ -98,11 +100,11 @@ def tile_attentionmm_pa_kernel(tc, x1, x2, W1, W2, b1, b2, out):
                 in_=w_sb[s][:, :, 256 * u : 256 * u + 256].rearrange("q s (p e) -> q e p s", e=2),
             )
 
-        def quantise_w(s):
+        def quantise_w(s, c0, c1):
             nc.vector.quantize_mx(
-                out=w_codes[s][:].bitcast(FP8X4),
-                scales=w_scales[s][:],
-                in_=wg[s][:].rearrange("q f s -> q (f s)"),
+                out=w_codes[s][:, c0:c1].bitcast(FP8X4),
+                scales=w_scales[s][:, c0:c1],
+                in_=wg[s][:, c0:c1, :].rearrange("q f s -> q (f s)"),
             )
 
         def transpose_pair(src, dst):
@@ -250,12 +252,13 @@ def tile_attentionmm_pa_kernel(tc, x1, x2, W1, W2, b1, b2, out):
         def last_slab_of(t):
             return 8 * (t // 8) + 4 + (t % 8) // 2
 
+        transpose_slab(0)
         regroup_w(1, 0, nc.vector.tensor_copy)
         regroup_w(1, 1, nc.vector.tensor_copy)
-        quantise_w(1)
-        transpose_slab(0)
-        transpose_slab(1)
+        quantise_w(1, 0, E // 2)
         quantise_x(0)
+        quantise_w(1, E // 2, E)
+        transpose_slab(1)
         project(0, 0)
         project(0, 1)
         transpose_slab(2)
@@ -302,7 +305,7 @@ def tile_attentionmm_pa_kernel(tc, x1, x2, W1, W2, b1, b2, out):
             if c == 1:
                 regroup_w(2, 1, nc.vector.tensor_copy)
             if c == 2:
-                quantise_w(2)
+                quantise_w(2, 0, E)
             if c == N_SLABS - 1:
                 quantise_e(c)
             for t in done:

from contextlib import ExitStack

import concourse.mybir as mybir
from concourse.masks import make_identity

F32 = mybir.dt.float32
BF16 = mybir.dt.bfloat16
U32 = mybir.dt.uint32
U8 = mybir.dt.uint8
FP8X4 = mybir.dt.float8_e4m3fn_x4
ALU = mybir.AluOpType
ACT = mybir.ActivationFunctionType
AX = mybir.AxisListType

B, T, E = 2, 1024, 512
P = 128
BANK = 512
SLAB = 256
N_SLABS = 2 * B * T // SLAB
N_ROW_TILES = B * T // P
FLOPS = 2 * (2 * B * T * E * E) + 2 * B * T * T * E

SCALAR_RELU_FROM = 5
VECTOR_SCALES_FROM = 12


def tile_attentionmm_pa_kernel(tc, x1, x2, W1, W2, b1, b2, out):
    nc = tc.nc
    with ExitStack() as ctx:
        ctx.enter_context(tc.manual_schedule())
        keep = ctx.enter_context(tc.tile_pool(name="keep", bufs=1))
        work = ctx.enter_context(tc.tile_pool(name="work", bufs=5))
        expool = ctx.enter_context(tc.tile_pool(name="expool", bufs=8))
        small = ctx.enter_context(tc.tile_pool(name="small", bufs=8))
        psum = ctx.enter_context(tc.psum_pool(name="psum", bufs=2))

        ws = {1: W1, 2: W2}
        x_view = {
            1: x1.rearrange("b (n p) k -> p b n k", p=P),
            2: x2.rearrange("b (p n) k -> p b n k", p=P),
        }
        b_view = {
            1: b1.rearrange("(n p) f -> p n f", p=P),
            2: b2.rearrange("(p n) f -> p n f", p=P),
        }
        out_view = out.rearrange("b (p n) j -> p b n j", p=P)

        x_sb, b_sb, w_sb, wg, w_codes, w_scales = {}, {}, {}, {}, {}, {}
        x_codes, x_scales, bT, e_codes, e_scales = {}, {}, {}, {}, {}
        for s in (1, 2):
            x_sb[s] = keep.tile([P, B, 8, E], BF16, name="x_sb%d" % s)
            b_sb[s] = keep.tile([P, 8, E], BF16, name="b_sb%d" % s)
            w_sb[s] = keep.tile([P, 4, E], BF16, name="w_sb%d" % s)
            wg[s] = keep.tile([P, E, 4], BF16, name="wg%d" % s, align_bytes=64)
            w_codes[s] = keep.tile([P, E], U32, name="w_codes%d" % s, align_bytes=64)
            w_scales[s] = keep.tile([P, E], U8, name="w_scales%d" % s, align_bytes=64)
            x_codes[s] = keep.tile([P, B * T], U32, name="x_codes%d" % s, align_bytes=64)
            x_scales[s] = keep.tile([P, B * T], U8, name="x_scales%d" % s, align_bytes=64)
            bT[s] = keep.tile([P, T, 4], BF16, name="bT%d" % s, align_bytes=64)
            e_codes[s] = keep.tile([P, B * T], U32, name="e_codes%d" % s, align_bytes=64)
            e_scales[s] = keep.tile([P, B * T], U8, name="e_scales%d" % s, align_bytes=64)

        def load_w(s, c0, c1):
            rows = ws[s].rearrange("(u q e) c -> q u e c", u=2, e=2)
            for u in range(2):
                nc.sync.dma_start(out=w_sb[s][:, 2 * u : 2 * u + 2, c0:c1], in_=rows[:, u, :, c0:c1])

        def load_x(s, b, n0, n1):
            nc.sync.dma_start(out=x_sb[s][:, b, n0:n1, :], in_=x_view[s][:, b, n0:n1, :])

        def load_b(s, n0, n1):
            nc.sync.dma_start(out=b_sb[s][:, n0:n1, :], in_=b_view[s][:, n0:n1, :])

        load_w(1, 0, E // 2)
        load_x(1, 0, 0, 2)
        load_w(1, E // 2, E)
        load_b(1, 0, 2)
        for q in range(1, 4):
            load_x(1, 0, 2 * q, 2 * q + 2)
            load_b(1, 2 * q, 2 * q + 2)
        load_w(2, 0, E)
        for half in range(2):
            load_x(2, 0, 4 * half, 4 * half + 4)
            load_b(2, 4 * half, 4 * half + 4)
        load_x(1, 1, 0, 8)
        load_x(2, 1, 0, 8)

        ident = keep.tile([P, P], F32, name="ident")
        make_identity(nc, ident[:])
        warm = keep.tile([P, 1], F32, name="warm")
        nc.vector.memset(warm[:], 0.0)
        nc.scalar.activation(out=warm[:], in_=warm[:], func=ACT.Exp)

        slabs = [(s, b, q) for b in range(B) for s in (1, 2) for q in range(4)]
        xg, pre, s1, sc, part, negm, ex, sums, tot, rs = {}, {}, {}, {}, {}, {}, {}, {}, {}, {}

        def regroup_w(s, u, copy):
            copy(
                out=wg[s][:, 256 * u : 256 * u + 256, :].rearrange("q (e p) s -> q e p s", e=2),
                in_=w_sb[s][:, :, 256 * u : 256 * u + 256].rearrange("q s (p e) -> q e p s", e=2),
            )

        def quantise_w(s, c0, c1):
            nc.vector.quantize_mx(
                out=w_codes[s][:, c0:c1].bitcast(FP8X4),
                scales=w_scales[s][:, c0:c1],
                in_=wg[s][:, c0:c1, :].rearrange("q f s -> q (f s)"),
            )

        def transpose_pair(src, dst):
            bank = psum.tile([P, BANK], F32, name="tp", tag="tp")
            planes = bank[:].rearrange("p (a u t) -> p a u t", a=2, u=2)
            for a in range(2):
                words = src[:, a, :].bitcast(F32)
                for u in range(2):
                    nc.tensor.transpose(planes[:, a, u, :], words[:, P * u : P * u + P], ident[:])
            nc.scalar.copy(
                out=dst.rearrange("p t j -> p (t j)").bitcast(F32).rearrange("p (a t u) -> p a t u", a=2, u=2),
                in_=planes.rearrange("p a u t -> p a t u"),
            )

        def transpose_slab(h):
            s, b, q = slabs[h]
            xg[h] = work.tile([P, SLAB, 4], BF16, name="xg", tag="xg", align_bytes=64)
            transpose_pair(x_sb[s][:, b, 2 * q : 2 * q + 2, :], xg[h][:])
            if b == 0:
                transpose_pair(b_sb[s][:, 2 * q : 2 * q + 2, :], bT[s][:, SLAB * q : SLAB * q + SLAB, :])

        def first_column(h):
            s, b, q = slabs[h]
            return b * T + q * SLAB

        def quantise_x(h):
            if h >= N_SLABS:
                return
            s = slabs[h][0]
            c0 = first_column(h)
            nc.vector.quantize_mx(
                out=x_codes[s][:, c0 : c0 + SLAB].bitcast(FP8X4),
                scales=x_scales[s][:, c0 : c0 + SLAB],
                in_=xg[h][:].rearrange("p t j -> p (t j)"),
            )

        def project(h, a):
            if h >= N_SLABS:
                return
            s = slabs[h][0]
            c0 = first_column(h) + P * a
            s1[h, a] = psum.tile([P, BANK], F32, name="s1", tag="s1")
            by_j = s1[h, a][:].rearrange("p (j t) -> p j t", j=4)
            for j in range(4):
                nc.tensor.matmul_mx(
                    out=by_j[:, j, :],
                    lhsT=w_codes[s][:, P * j : P * j + P].bitcast(FP8X4),
                    lhsT_scale=w_scales[s][:, P * j : P * j + P],
                    rhs=x_codes[s][:, c0 : c0 + P].bitcast(FP8X4),
                    rhs_scale=x_scales[s][:, c0 : c0 + P],
                    start=True,
                    stop=True,
                )

        def add_bias(h, a):
            s, b, q = slabs[h]
            if a == 0:
                pre[h] = work.tile([P, SLAB, 4], BF16, name="pre", tag="pre", align_bytes=64)
            nc.vector.tensor_tensor(
                out=pre[h][:, P * a : P * a + P, :],
                in0=s1[h, a][:].rearrange("p (j t) -> p t j", j=4),
                in1=bT[s][:, SLAB * q + P * a : SLAB * q + P * a + P, :],
                op=ALU.add,
            )

        def relu(h):
            flat = pre[h][:].rearrange("p t j -> p (t j)")
            if h >= SCALAR_RELU_FROM:
                nc.scalar.activation(out=flat, in_=flat, func=ACT.Relu)
            else:
                nc.vector.tensor_scalar_max(out=flat, in0=flat, scalar1=0.0)

        def quantise_e(h):
            if h < 0:
                return
            s = slabs[h][0]
            c0 = first_column(h)
            nc.vector.quantize_mx(
                out=e_codes[s][:, c0 : c0 + SLAB].bitcast(FP8X4),
                scales=e_scales[s][:, c0 : c0 + SLAB],
                in_=pre[h][:].rearrange("p t j -> p (t j)"),
            )

        def scores(t):
            tag = {N_ROW_TILES - 2: "tp", N_ROW_TILES - 1: "s1"}.get(t, "sc")
            for hh in range(2):
                sc[t, hh] = psum.tile([P, BANK], F32, name="sc", tag=tag, bufs=4 if tag == "sc" else 2)
                j0 = (t // 8) * T + BANK * hh
                nc.tensor.matmul_mx(
                    out=sc[t, hh][:],
                    lhsT=e_codes[2][:, P * t : P * t + P].bitcast(FP8X4),
                    lhsT_scale=e_scales[2][:, P * t : P * t + P],
                    rhs=e_codes[1][:, j0 : j0 + BANK].bitcast(FP8X4),
                    rhs_scale=e_scales[1][:, j0 : j0 + BANK],
                    start=True,
                    stop=True,
                )

        def bank_max(t, hh):
            if hh == 0:
                part[t] = small.tile([P, 2], F32, name="part", tag="part")
            nc.vector.tensor_reduce(out=part[t][:, hh : hh + 1], in_=sc[t, hh][:], axis=AX.X, op=ALU.max)

        def row_max(t):
            negm[t] = small.tile([P, 1], F32, name="negm", tag="negm")
            nc.vector.tensor_reduce(out=negm[t][:], in_=part[t][:], axis=AX.X, op=ALU.max, negate=True)

        def exponent(t):
            ex[t] = expool.tile([P, T], F32, name="ex", tag="ex")
            sums[t] = small.tile([P, 2], F32, name="sums", tag="sums")
            for hh in range(2):
                nc.scalar.activation(
                    out=ex[t][:, BANK * hh : BANK * hh + BANK],
                    in_=sc[t, hh][:],
                    func=ACT.Exp,
                    bias=negm[t][:, 0:1],
                    scale=1.0,
                    accum_out=sums[t][:, hh : hh + 1],
                )

        def row_sum(t):
            tot[t] = small.tile([P, 1], F32, name="tot", tag="tot")
            nc.vector.tensor_reduce(out=tot[t][:], in_=sums[t][:], axis=AX.X, op=ALU.add)

        def inverse(t):
            rs[t] = small.tile([P, 1], F32, name="rs", tag="rs")
            nc.vector.reciprocal(out=rs[t][:], in_=tot[t][:])

        def scale_and_store(t):
            if t >= VECTOR_SCALES_FROM:
                nc.vector.tensor_scalar_mul(out=ex[t][:], in0=ex[t][:], scalar1=rs[t][:, 0:1])
            else:
                nc.gpsimd.tensor_scalar(
                    out=ex[t][:], in0=ex[t][:], scalar1=rs[t][:, 0:1], scalar2=0.0, op0=ALU.mult, op1=ALU.add
                )
            nc.sync.dma_start(out=out_view[:, t // 8, t % 8, :], in_=ex[t][:])

        def row_tiles_of(c):
            if c < 6:
                return []
            if c < 14:
                return [c - 6]
            return [2 * c - 20, 2 * c - 19]

        def last_slab_of(t):
            return 8 * (t // 8) + 4 + (t % 8) // 2

        transpose_slab(0)
        regroup_w(1, 0, nc.vector.tensor_copy)
        regroup_w(1, 1, nc.vector.tensor_copy)
        quantise_w(1, 0, E // 2)
        quantise_x(0)
        quantise_w(1, E // 2, E)
        transpose_slab(1)
        project(0, 0)
        project(0, 1)
        transpose_slab(2)
        transposed = 3

        for c in range(N_SLABS):
            tiles = row_tiles_of(c)
            two = len(tiles) == 2
            done = [t for t in range(tiles[0] - 1, tiles[-1]) if t >= 0] if tiles else []
            fresh = bool(tiles) and last_slab_of(tiles[0]) == c - 2

            add_bias(c, 0)
            if c == 0:
                quantise_x(1)
            project(c + 1, 0)
            if tiles and not fresh:
                bank_max(tiles[0], 0)
            add_bias(c, 1)
            project(c + 1, 1)
            if fresh:
                bank_max(tiles[0], 0)
            if c >= SCALAR_RELU_FROM:
                relu(c)
            if tiles:
                bank_max(tiles[0], 1)
            if two:
                bank_max(tiles[1], 0)

            quantise_x(c + 2)
            if c < SCALAR_RELU_FROM:
                relu(c)
            if tiles:
                row_max(tiles[0])
                exponent(tiles[0])
            if two:
                bank_max(tiles[1], 1)
            if done:
                row_sum(done[0])
            quantise_e(c - 1)
            if two:
                row_max(tiles[1])
                exponent(tiles[1])
                row_sum(done[1])
            if c == 1:
                regroup_w(2, 1, nc.vector.tensor_copy)
            if c == 2:
                quantise_w(2, 0, E)
            if c == N_SLABS - 1:
                quantise_e(c)
            for t in done:
                inverse(t)
            for t in done:
                scale_and_store(t)
            if c == 1:
                regroup_w(2, 0, nc.scalar.copy)

            ahead = 3 if c < 5 else 4
            while transposed < min(N_SLABS, c + ahead + 1):
                transpose_slab(transposed)
                transposed += 1
            for t in row_tiles_of(c + 1):
                scores(t)

        scores(14)
        scores(15)
        bank_max(12, 0)
        bank_max(12, 1)
        row_sum(11)
        row_max(12)
        exponent(12)
        inverse(11)
        scale_and_store(11)
        bank_max(13, 0)
        bank_max(13, 1)
        for t in (14, 15):
            bank_max(t, 0)
            row_max(t - 1)
            exponent(t - 1)
            bank_max(t, 1)
            row_sum(t - 2)
        row_max(15)
        exponent(15)
        for t in (12, 13):
            inverse(t)
        for t in (12, 13):
            scale_and_store(t)
        for t in (14, 15):
            row_sum(t)
            inverse(t)
            scale_and_store(t)
